import numpy as np
import ml_dtypes


def mxq(x, axis, fmt="e4m3"):
    dtype, down = {"e4m3": (ml_dtypes.float8_e4m3fn, 7), "e5m2": (ml_dtypes.float8_e5m2, 14)}[fmt]
    v = np.moveaxis(np.asarray(x, np.float32).astype(ml_dtypes.bfloat16).astype(np.float64), axis, -1)
    blocks = v.reshape(v.shape[:-1] + (-1, 32))
    amax = np.abs(blocks).max(-1, keepdims=True)
    byte = np.maximum(np.where(amax > 0, np.frexp(amax)[1] - 1 + 127, 0) - down, 1)
    scale = np.exp2(byte - 127.0)
    codes = (blocks / scale).astype(np.float32).astype(dtype).astype(np.float64)
    return np.moveaxis((codes * scale).reshape(v.shape), -1, axis)


WIDE = False


def mx_kscale(k):
    if not WIDE:
        return np.ones(k)
    levels = np.array([10, -10, 5, -5, 0])
    a = np.random.permutation(np.resize(levels, k // 512 * 4)).reshape(k // 512, 4)
    idx = np.arange(k)
    return np.exp2(a[idx // 512, idx % 128 // 32])


BF16 = ml_dtypes.bfloat16


def bf(x):
    return np.asarray(x, np.float32).astype(BF16)


def f64(x):
    return np.asarray(x).astype(np.float64)


E2M1 = np.array([0.0, 0.5, 1.0, 1.5, 2.0, 3.0, 4.0, 6.0, -0.0, -0.5, -1.0, -1.5, -2.0, -3.0, -4.0, -6.0])


def pack_weight(w, fmt):
    k, n = w.shape
    w = f64(bf(w)).reshape(k // 32, 32, n)
    amax = np.abs(w).max(1)
    if fmt == "e4m3":
        byte = np.frexp(amax)[1] - 1 + 127 - 7
    else:
        mant, ex = np.frexp(amax / 6.0)
        byte = np.where(mant > 0.5, ex, ex - 1) + 127
    byte = np.clip(np.where(amax > 0, byte, 1), 1, 254)
    scaled = (w * np.exp2(127.0 - byte)[:, None, :]).reshape(k, n).astype(np.float32)
    by_word = np.ascontiguousarray(scaled.reshape(k // 512, 128, 4, n).transpose(0, 1, 3, 2))
    if fmt == "e4m3":
        words = by_word.astype(ml_dtypes.float8_e4m3fn).view(np.uint8)
    else:
        c = by_word.astype(ml_dtypes.float4_e2m1fn).view(np.uint8) & 0xF
        words = c[..., 0::2] | (c[..., 1::2] << 4)
    return np.ascontiguousarray(words), np.ascontiguousarray(byte.astype(np.uint8).reshape(k // 512, 16, n))


def unpack_weight(words, scales, fmt):
    g, p, n, _ = words.shape
    if fmt == "e4m3":
        vals = np.ascontiguousarray(words).view(ml_dtypes.float8_e4m3fn).astype(np.float64)
    else:
        nib = np.empty((g, p, n, 4), np.uint8)
        nib[..., 0::2] = words & 0xF
        nib[..., 1::2] = words >> 4
        vals = E2M1[nib]
    vals = vals * np.repeat(np.exp2(scales.astype(np.float64) - 127.0), 8, axis=1)[..., None]
    return vals.transpose(0, 1, 3, 2).reshape(g * 512, n)

def pack4(w):
    words, scales = pack_weight(w, "e2m1")
    return words.reshape(words.shape[0], 128, -1), scales


def unpack4(words, scales):
    return unpack_weight(words.reshape(words.shape[0], 128, -1, 2), scales, "e2m1")


B, C, HH, WW, NH, HD, F = 4, 512, 16, 16, 8, 64, 2048
EPS = 1e-5


def layer_norm(v, w, b):
    mu = v.mean(-1, keepdims=True)
    var = ((v - mu) ** 2).mean(-1, keepdims=True)
    return (v - mu) * (1.0 / np.sqrt(var + EPS)) * w + b


def setup_inputs():
    s = mx_kscale(F)
    h = bf(np.maximum(np.random.standard_normal((B, HH, WW, F)), 0.0) * 0.125 * s)
    ffn2_w = np.random.standard_normal((C, F)) * 0.5 / np.sqrt(F) / s
    words, scales = pack4(np.ascontiguousarray(ffn2_w.T))
    return {"h": h,
            "ffn2_w_words": words,
            "ffn2_w_scales": scales,
            "ffn2_b": bf(np.random.standard_normal(C) * 0.02),
            "scale_ffn": bf(0.1 * (1.0 + 0.1 * np.random.standard_normal(1))),
            "ln2_w": bf(1.0 + 0.1 * np.random.standard_normal(C)),
            "ln2_b": bf(0.1 * np.random.standard_normal(C)),
            "scale_norm2": bf(1.5 * (1.0 + 0.1 * np.random.standard_normal(1))),
            "x": bf(np.random.standard_normal((B, C, HH, WW)))}


def reference(h, ffn2_w_words, ffn2_w_scales, ffn2_b, scale_ffn, ln2_w, ln2_b, scale_norm2, x):
    y2 = ((mxq(f64(h), 3, "e4m3") @ unpack4(ffn2_w_words, ffn2_w_scales)) + f64(ffn2_b)) * f64(scale_ffn)
    y2 = layer_norm(y2, f64(ln2_w), f64(ln2_b)) * f64(scale_norm2)
    out = np.maximum(y2 + f64(x).transpose(0, 2, 3, 1), 0.0)
    return out.transpose(0, 3, 1, 2)

@@ -1,0 +1,247 @@
+from contextlib import ExitStack
+
+import concourse.mybir as mybir
+from concourse.masks import make_identity
+
+F32 = mybir.dt.float32
+BF16 = mybir.dt.bfloat16
+I32 = mybir.dt.int32
+U32 = mybir.dt.uint32
+U8 = mybir.dt.uint8
+FP8X4 = mybir.dt.float8_e4m3fn_x4
+FP4X4 = mybir.dt.float4_e2m1fn_x4
+ALU = mybir.AluOpType
+ACT = mybir.ActivationFunctionType
+
+P = 128
+PACK = 4
+K_PASS = P * PACK
+K = 2048
+PASSES = K // K_PASS
+CHANNELS = 512
+CH_PER_PART = CHANNELS // P
+BATCH = 4
+IMAGE = 256
+TILES = BATCH * IMAGE // P
+TILES_PER_IMAGE = IMAGE // P
+WORDS_PASS = K_PASS // 2
+PASSES_PER_BANK = 2
+EPS = 1e-5
+
+FLOPS = 2 * BATCH * IMAGE * K * CHANNELS
+
+
+def tile_transformerconvblock_pc_kernel(
+    tc, h, ffn2_w_words, ffn2_w_scales, ffn2_b, scale_ffn, ln2_w, ln2_b, scale_norm2, x, out
+):
+    nc = tc.nc
+    h_rows = h.rearrange("b i j k -> (b i j) k")
+    x_view = x.rearrange("b (cc j) i w -> cc b (j i w)", j=CH_PER_PART)
+    out_view = out.rearrange("b (cc j) i w -> b cc (j i w)", j=CH_PER_PART)
+
+    with ExitStack() as ctx:
+        const = ctx.enter_context(tc.tile_pool(name="const", bufs=1))
+        h_pool = ctx.enter_context(tc.tile_pool(name="h", bufs=TILES))
+        work = ctx.enter_context(tc.tile_pool(name="work", bufs=3))
+        stats = ctx.enter_context(tc.tile_pool(name="stats", bufs=3))
+        ps_h = ctx.enter_context(tc.psum_pool(name="ps_h", bufs=2))
+        ps_acc = ctx.enter_context(tc.psum_pool(name="ps_acc", bufs=2))
+        ps_n = ctx.enter_context(tc.psum_pool(name="ps_n", bufs=2))
+
+        h_sb = {}
+
+        def load_h(t):
+            h_tile = h_pool.tile([P, K], BF16)
+            nc.sync.dma_start(out=h_tile[:], in_=h_rows[t * P : (t + 1) * P, :])
+            h_sb[t] = h_tile
+
+        load_h(0)
+        load_h(1)
+
+        w_words = const.tile([P, PASSES, 2 * CHANNELS], U8, align_bytes=64)
+        nc.sync.dma_start(out=w_words[:].bitcast(I32), in_=ffn2_w_words.bitcast(I32).rearrange("g p n -> p g n"))
+
+        w_scales = const.tile([P, PASSES, CHANNELS], U8, align_bytes=64)
+        nc.vector.memset(w_scales[:].rearrange("p g n -> p (g n)").bitcast(I32), 0)
+        scale_rows = ffn2_w_scales.bitcast(I32)
+        for quad in range(4):
+            nc.sync.dma_start(
+                out=w_scales[32 * quad : 32 * quad + 4, :, :].bitcast(I32),
+                in_=scale_rows[:, 4 * quad : 4 * quad + 4, :].rearrange("g r n -> r g n"),
+            )
+        for t in range(2, TILES):
+            load_h(t)
+
+        bias_row = const.tile([P, CHANNELS], BF16)
+        nc.vector.memset(bias_row[:], 0.0)
+        nc.scalar.dma_start(out=bias_row[0:1, :], in_=ffn2_b.unsqueeze(0))
+        s_ffn = const.tile([P, 1], BF16)
+        nc.scalar.dma_start(out=s_ffn[:], in_=scale_ffn.partition_broadcast(P))
+        s_norm = const.tile([P, 1], BF16)
+        nc.scalar.dma_start(out=s_norm[:], in_=scale_norm2.partition_broadcast(P))
+        ln_w = const.tile([P, CH_PER_PART], BF16)
+        nc.scalar.dma_start(out=ln_w[:], in_=ln2_w.rearrange("(cc j) -> cc j", j=CH_PER_PART))
+        ln_b = const.tile([P, CH_PER_PART], BF16)
+        nc.scalar.dma_start(out=ln_b[:], in_=ln2_b.rearrange("(cc j) -> cc j", j=CH_PER_PART))
+
+        ident = const.tile([P, P], F32)
+        nc.vector.memset(ident[:], 0.0)
+        make_identity(nc, ident[:], nomemset=True)
+        x_sb = const.tile([P, BATCH, CH_PER_PART * IMAGE], BF16)
+        nc.gpsimd.dma_start(out=x_sb[:], in_=x_view)
+
+        one = const.tile([P, 1], F32)
+        nc.vector.memset(one[:], 1.0)
+        table_warm = const.tile([P, 1], F32)
+        nc.scalar.activation(out=table_warm[:], in_=one[:], func=ACT.Sqrt)
+
+        ones = const.tile([P, P], BF16)
+        nc.vector.memset(ones[:], 1.0)
+        bias_ps = ps_acc.tile([P, CHANNELS], F32, tag="acc")
+        nc.tensor.matmul(out=bias_ps[:], lhsT=ones[:], rhs=bias_row[:], start=True, stop=True)
+        bias_all = const.tile([P, CH_PER_PART, P], F32)
+        nc.vector.tensor_copy(out=bias_all[:], in_=bias_ps[:].rearrange("p (cc j) -> p j cc", j=CH_PER_PART))
+
+        var_scale = const.tile([P, 1], F32)
+        nc.vector.tensor_scalar(
+            out=var_scale[:], in0=s_ffn[:], scalar1=s_ffn[:, 0:1], scalar2=1.0 / CHANNELS, op0=ALU.mult, op1=ALU.mult
+        )
+        gain = const.tile([P, CH_PER_PART], F32)
+        nc.vector.tensor_scalar(
+            out=gain[:], in0=ln_w[:], scalar1=s_norm[:, 0:1], scalar2=s_ffn[:, 0:1], op0=ALU.mult, op1=ALU.mult
+        )
+        shift = const.tile([P, CH_PER_PART], F32)
+        nc.vector.tensor_scalar(out=shift[:], in0=ln_b[:], scalar1=s_norm[:, 0:1], scalar2=None, op0=ALU.mult)
+
+        grouped_of, codes_of, planes_of, acc_of = {}, {}, {}, {}
+        v_of, neg_mean_of, dev_of, n_of, n_t_of = {}, {}, {}, {}, {}
+
+        def transpose_h(t, bank):
+            if bank == 0:
+                grouped = work.tile([P, K], BF16, align_bytes=64)
+                grouped_of[t] = grouped
+            h_words = h_sb[t][:].bitcast(F32)
+            h_t = ps_h.tile([P, PASSES_PER_BANK, 2, P], F32)
+            for gg in range(PASSES_PER_BANK):
+                first = (bank * PASSES_PER_BANK + gg) * WORDS_PASS
+                for u in range(2):
+                    nc.tensor.transpose(h_t[:, gg, u, :], h_words[:, first + u : first + WORDS_PASS : 2], ident[:])
+            width = PASSES_PER_BANK * WORDS_PASS
+            nc.scalar.copy(
+                out=grouped_of[t][:]
+                .bitcast(F32)[:, bank * width : (bank + 1) * width]
+                .rearrange("p (g r u) -> p g r u", g=PASSES_PER_BANK, u=2),
+                in_=h_t[:].rearrange("p g u r -> p g r u"),
+            )
+
+        def quantise_h(t):
+            codes = work.tile([P, PASSES * P], U32, align_bytes=64)
+            planes = work.tile([P, PASSES * P], U8, align_bytes=64)
+            nc.vector.quantize_mx(out=codes[:].bitcast(FP8X4), scales=planes[:], in_=grouped_of[t][:])
+            codes_of[t], planes_of[t] = codes, planes
+
+        def multiply(t):
+            acc = ps_acc.tile([P, CHANNELS], F32, tag="acc")
+            for g in range(PASSES):
+                pixels = slice(g * P, (g + 1) * P)
+                nc.tensor.matmul_mx(
+                    out=acc[:],
+                    lhsT=codes_of[t][:, pixels].bitcast(FP8X4),
+                    lhsT_scale=planes_of[t][:, pixels],
+                    rhs=w_words[:, g, :].bitcast(FP4X4),
+                    rhs_scale=w_scales[:, g, :],
+                    start=(g == 0),
+                    stop=(g == PASSES - 1),
+                )
+            acc_of[t] = acc
+
+        def add_bias(t):
+            v = work.tile([P, CH_PER_PART, P], F32)
+            v_sum = stats.tile([P, 1], F32)
+            nc.vector.scalar_tensor_tensor(
+                out=v[:],
+                in0=acc_of[t][:].rearrange("p (cc j) -> p j cc", j=CH_PER_PART),
+                scalar=1.0,
+                in1=bias_all[:],
+                op0=ALU.mult,
+                op1=ALU.add,
+                accum_out=v_sum[:],
+            )
+            neg_mean = stats.tile([P, 1], F32)
+            nc.vector.tensor_scalar(out=neg_mean[:], in0=v_sum[:], scalar1=-1.0 / CHANNELS, scalar2=None, op0=ALU.mult)
+            v_of[t], neg_mean_of[t] = v, neg_mean
+
+        def deviation(t):
+            squares = work.tile([P, CHANNELS], F32)
+            sq_sum = stats.tile([P, 1], F32)
+            nc.scalar.activation(
+                out=squares[:],
+                in_=v_of[t][:].rearrange("p j cc -> p (j cc)"),
+                func=ACT.Square,
+                bias=neg_mean_of[t][:, 0:1],
+                scale=1.0,
+                accum_out=sq_sum[:],
+            )
+            dev = stats.tile([P, 1], F32)
+            nc.scalar.activation(out=dev[:], in_=sq_sum[:], func=ACT.Sqrt, bias=EPS, scale=var_scale[:, 0:1])
+            dev_of[t] = dev
+
+        def normalise(t):
+            inv_dev = stats.tile([P, 1], F32)
+            nc.vector.reciprocal(out=inv_dev[:], in_=dev_of[t][:])
+            n = work.tile([P, CH_PER_PART, P], F32)
+            nc.vector.tensor_scalar(
+                out=n[:].rearrange("p j cc -> p (j cc)"),
+                in0=v_of[t][:].rearrange("p j cc -> p (j cc)"),
+                scalar1=neg_mean_of[t][:, 0:1],
+                scalar2=inv_dev[:, 0:1],
+                op0=ALU.add,
+                op1=ALU.mult,
+            )
+            n_of[t] = n
+
+        def transpose_n(t):
+            image, half = divmod(t, TILES_PER_IMAGE)
+            if half == 0:
+                n_t_lo = ps_n.tile([P, 2, IMAGE], F32)
+                n_t_hi = ps_n.tile([P, 2, IMAGE], F32)
+                n_t_of[image] = (n_t_lo, n_t_hi)
+            for j in range(CH_PER_PART):
+                nc.tensor.transpose(n_t_of[image][j // 2][:, j % 2, half * P : (half + 1) * P], n_of[t][:, j, :], ident[:])
+
+        def finish(image):
+            res = work.tile([P, CH_PER_PART, IMAGE], F32)
+            for j in range(CH_PER_PART):
+                nc.vector.scalar_tensor_tensor(
+                    out=res[:, j, :],
+                    in0=n_t_of[image][j // 2][:, j % 2, :],
+                    scalar=gain[:, j : j + 1],
+                    in1=x_sb[:, image, j * IMAGE : (j + 1) * IMAGE],
+                    op0=ALU.mult,
+                    op1=ALU.add,
+                )
+                nc.scalar.activation(
+                    out=res[:, j, :], in_=res[:, j, :], func=ACT.Relu, bias=shift[:, j : j + 1], scale=1.0
+                )
+            nc.sync.dma_start(out=out_view[image], in_=res[:].rearrange("p j w -> p (j w)"))
+
+        for r in range(-1, TILES + 2):
+            ahead, norm, back = r + 1, r - 1, r - 2
+            if 0 <= norm < TILES:
+                add_bias(norm)
+            if ahead < TILES:
+                transpose_h(ahead, 0)
+            if 0 <= norm < TILES:
+                deviation(norm)
+            if ahead < TILES:
+                transpose_h(ahead, 1)
+            if 0 <= back < TILES:
+                transpose_n(back)
+            if 0 <= r < TILES:
+                multiply(r)
+            if 0 <= back < TILES and back % TILES_PER_IMAGE == TILES_PER_IMAGE - 1:
+                finish(back // TILES_PER_IMAGE)
+            if 0 <= norm < TILES:
+                normalise(norm)
+            if ahead < TILES:
+                quantise_h(ahead)

@@ -225,23 +225,24 @@ def tile_transformerconvblock_pc_kernel(
                 )
             nc.sync.dma_start(out=out_view[image], in_=res[:].rearrange("p j w -> p (j w)"))
 
-        for r in range(-1, TILES + 2):
-            ahead, norm, back = r + 1, r - 1, r - 2
-            if 0 <= norm < TILES:
-                add_bias(norm)
-            if ahead < TILES:
-                transpose_h(ahead, 0)
-            if 0 <= norm < TILES:
-                deviation(norm)
-            if ahead < TILES:
-                transpose_h(ahead, 1)
-            if 0 <= back < TILES:
-                transpose_n(back)
-            if 0 <= r < TILES:
-                multiply(r)
-            if 0 <= back < TILES and back % TILES_PER_IMAGE == TILES_PER_IMAGE - 1:
-                finish(back // TILES_PER_IMAGE)
-            if 0 <= norm < TILES:
-                normalise(norm)
-            if ahead < TILES:
-                quantise_h(ahead)
+        with tc.manual_schedule():
+            for r in range(-1, TILES + 2):
+                ahead, norm, back = r + 1, r - 1, r - 2
+                if 0 <= norm < TILES:
+                    add_bias(norm)
+                if ahead < TILES:
+                    transpose_h(ahead, 0)
+                if 0 <= norm < TILES:
+                    deviation(norm)
+                if ahead < TILES:
+                    transpose_h(ahead, 1)
+                if 0 <= back < TILES:
+                    transpose_n(back)
+                if 0 <= r < TILES:
+                    multiply(r)
+                if 0 <= back < TILES and back % TILES_PER_IMAGE == TILES_PER_IMAGE - 1:
+                    finish(back // TILES_PER_IMAGE)
+                if 0 <= norm < TILES:
+                    normalise(norm)
+                if ahead < TILES:
+                    quantise_h(ahead)

@@ -1,7 +1,6 @@
 from contextlib import ExitStack
 
 import concourse.mybir as mybir
-from concourse.masks import make_identity
 
 F32 = mybir.dt.float32
 BF16 = mybir.dt.bfloat16
@@ -26,6 +25,8 @@ TILES = BATCH * IMAGE // P
 TILES_PER_IMAGE = IMAGE // P
 WORDS_PASS = K_PASS // 2
 PASSES_PER_BANK = 2
+BLOCK = 32
+LEAD = 2
 EPS = 1e-5
 
 FLOPS = 2 * BATCH * IMAGE * K * CHANNELS
@@ -36,23 +37,43 @@ def tile_transformerconvblock_pc_kernel(
 ):
     nc = tc.nc
     h_rows = h.rearrange("b i j k -> (b i j) k")
-    x_view = x.rearrange("b (cc j) i w -> cc b (j i w)", j=CH_PER_PART)
-    out_view = out.rearrange("b (cc j) i w -> b cc (j i w)", j=CH_PER_PART)
+    x_view = x.rearrange("b (cc j) i w -> cc b j (i w)", j=CH_PER_PART)
+    out_view = out.rearrange("b (cc j) i w -> b cc j (i w)", j=CH_PER_PART)
 
     with ExitStack() as ctx:
         const = ctx.enter_context(tc.tile_pool(name="const", bufs=1))
         h_pool = ctx.enter_context(tc.tile_pool(name="h", bufs=TILES))
         work = ctx.enter_context(tc.tile_pool(name="work", bufs=3))
         stats = ctx.enter_context(tc.tile_pool(name="stats", bufs=3))
-        ps_h = ctx.enter_context(tc.psum_pool(name="ps_h", bufs=2))
+        ps_h = ctx.enter_context(tc.psum_pool(name="ps_h", bufs=4))
         ps_acc = ctx.enter_context(tc.psum_pool(name="ps_acc", bufs=2))
         ps_n = ctx.enter_context(tc.psum_pool(name="ps_n", bufs=2))
+
+        w_scales = const.tile([P, PASSES, CHANNELS], U8, align_bytes=64)
+        nc.vector.memset(w_scales[:].rearrange("p g n -> p (g n)").bitcast(I32), 0)
+
+        col = const.tile([P, BLOCK], F32, align_bytes=64)
+        for c in range(4):
+            nc.vector.memset(col[:, c : c + 1], float(c))
+        for width in (4, 8, 16):
+            nc.vector.tensor_scalar_add(out=col[:, width : 2 * width], in0=col[:, 0:width], scalar1=float(width))
+        row = const.tile([P, BLOCK], F32, align_bytes=64)
+        nc.vector.transpose(out=row[:], in_=col[:])
+        diagonal = const.tile([P, BLOCK], F32)
+        nc.vector.tensor_tensor(out=diagonal[:], in0=col[:], in1=row[:], op=ALU.is_equal)
+        ident = const.tile([P, P], F32)
+        nc.vector.memset(ident[:], 0.0)
+        for first in range(0, P, BLOCK):
+            block = slice(first, first + BLOCK)
+            nc.vector.tensor_copy(out=ident[block, block], in_=diagonal[block, :])
 
         h_sb = {}
 
         def load_h(t):
             h_tile = h_pool.tile([P, K], BF16)
-            nc.sync.dma_start(out=h_tile[:], in_=h_rows[t * P : (t + 1) * P, :])
+            for half in range(2):
+                cols = slice(half * K // 2, (half + 1) * K // 2)
+                nc.sync.dma_start(out=h_tile[:, cols], in_=h_rows[t * P : (t + 1) * P, cols])
             h_sb[t] = h_tile
 
         load_h(0)
@@ -61,15 +82,16 @@ def tile_transformerconvblock_pc_kernel(
         w_words = const.tile([P, PASSES, 2 * CHANNELS], U8, align_bytes=64)
         nc.sync.dma_start(out=w_words[:].bitcast(I32), in_=ffn2_w_words.bitcast(I32).rearrange("g p n -> p g n"))
 
-        w_scales = const.tile([P, PASSES, CHANNELS], U8, align_bytes=64)
-        nc.vector.memset(w_scales[:].rearrange("p g n -> p (g n)").bitcast(I32), 0)
         scale_rows = ffn2_w_scales.bitcast(I32)
         for quad in range(4):
             nc.sync.dma_start(
                 out=w_scales[32 * quad : 32 * quad + 4, :, :].bitcast(I32),
                 in_=scale_rows[:, 4 * quad : 4 * quad + 4, :].rearrange("g r n -> r g n"),
             )
-        for t in range(2, TILES):
+        load_h(2)
+        x_sb = const.tile([P, BATCH, CH_PER_PART, IMAGE], BF16)
+        nc.sync.dma_start(out=x_sb[:], in_=x_view)
+        for t in range(3, TILES):
             load_h(t)
 
         bias_row = const.tile([P, CHANNELS], BF16)
@@ -84,23 +106,11 @@ def tile_transformerconvblock_pc_kernel(
         ln_b = const.tile([P, CH_PER_PART], BF16)
         nc.scalar.dma_start(out=ln_b[:], in_=ln2_b.rearrange("(cc j) -> cc j", j=CH_PER_PART))
 
-        ident = const.tile([P, P], F32)
-        nc.vector.memset(ident[:], 0.0)
-        make_identity(nc, ident[:], nomemset=True)
-        x_sb = const.tile([P, BATCH, CH_PER_PART * IMAGE], BF16)
-        nc.gpsimd.dma_start(out=x_sb[:], in_=x_view)
 
         one = const.tile([P, 1], F32)
         nc.vector.memset(one[:], 1.0)
         table_warm = const.tile([P, 1], F32)
         nc.scalar.activation(out=table_warm[:], in_=one[:], func=ACT.Sqrt)
-
-        ones = const.tile([P, P], BF16)
-        nc.vector.memset(ones[:], 1.0)
-        bias_ps = ps_acc.tile([P, CHANNELS], F32, tag="acc")
-        nc.tensor.matmul(out=bias_ps[:], lhsT=ones[:], rhs=bias_row[:], start=True, stop=True)
-        bias_all = const.tile([P, CH_PER_PART, P], F32)
-        nc.vector.tensor_copy(out=bias_all[:], in_=bias_ps[:].rearrange("p (cc j) -> p j cc", j=CH_PER_PART))
 
         var_scale = const.tile([P, 1], F32)
         nc.vector.tensor_scalar(
@@ -201,48 +211,58 @@ def tile_transformerconvblock_pc_kernel(
             n_of[t] = n
 
         def transpose_n(t):
-            image, half = divmod(t, TILES_PER_IMAGE)
-            if half == 0:
-                n_t_lo = ps_n.tile([P, 2, IMAGE], F32)
-                n_t_hi = ps_n.tile([P, 2, IMAGE], F32)
-                n_t_of[image] = (n_t_lo, n_t_hi)
+            n_t = ps_n.tile([P, CH_PER_PART, P], F32)
             for j in range(CH_PER_PART):
-                nc.tensor.transpose(n_t_of[image][j // 2][:, j % 2, half * P : (half + 1) * P], n_of[t][:, j, :], ident[:])
+                nc.tensor.transpose(n_t[:, j, :], n_of[t][:, j, :], ident[:])
+            n_t_of[t] = n_t
 
-        def finish(image):
-            res = work.tile([P, CH_PER_PART, IMAGE], F32)
+        def finish(t):
+            image, half = divmod(t, TILES_PER_IMAGE)
+            pixels = slice(half * P, (half + 1) * P)
+            res = work.tile([P, CH_PER_PART, P], F32)
             for j in range(CH_PER_PART):
                 nc.vector.scalar_tensor_tensor(
                     out=res[:, j, :],
-                    in0=n_t_of[image][j // 2][:, j % 2, :],
+                    in0=n_t_of[t][:, j, :],
                     scalar=gain[:, j : j + 1],
-                    in1=x_sb[:, image, j * IMAGE : (j + 1) * IMAGE],
+                    in1=x_sb[:, image, j, pixels],
                     op0=ALU.mult,
                     op1=ALU.add,
                 )
                 nc.scalar.activation(
                     out=res[:, j, :], in_=res[:, j, :], func=ACT.Relu, bias=shift[:, j : j + 1], scale=1.0
                 )
-            nc.sync.dma_start(out=out_view[image], in_=res[:].rearrange("p j w -> p (j w)"))
+            nc.sync.dma_start(out=out_view[image][:, :, pixels], in_=res[:])
 
-        with tc.manual_schedule():
-            for r in range(-1, TILES + 2):
-                ahead, norm, back = r + 1, r - 1, r - 2
-                if 0 <= norm < TILES:
-                    add_bias(norm)
-                if ahead < TILES:
-                    transpose_h(ahead, 0)
-                if 0 <= norm < TILES:
-                    deviation(norm)
-                if ahead < TILES:
-                    transpose_h(ahead, 1)
-                if 0 <= back < TILES:
-                    transpose_n(back)
-                if 0 <= r < TILES:
-                    multiply(r)
-                if 0 <= back < TILES and back % TILES_PER_IMAGE == TILES_PER_IMAGE - 1:
-                    finish(back // TILES_PER_IMAGE)
-                if 0 <= norm < TILES:
-                    normalise(norm)
-                if ahead < TILES:
-                    quantise_h(ahead)
+        for t in range(LEAD):
+            transpose_h(t, 0)
+            transpose_h(t, 1)
+            quantise_h(t)
+
+        ones = const.tile([P, P], BF16)
+        nc.vector.memset(ones[:], 1.0)
+        bias_ps = ps_acc.tile([P, CHANNELS], F32, tag="acc")
+        nc.tensor.matmul(out=bias_ps[:], lhsT=ones[:], rhs=bias_row[:], start=True, stop=True)
+        bias_all = const.tile([P, CH_PER_PART, P], F32)
+        nc.vector.tensor_copy(out=bias_all[:], in_=bias_ps[:].rearrange("p (cc j) -> p j cc", j=CH_PER_PART))
+
+        for r in range(TILES + 2):
+            ahead, norm, back = r + LEAD, r - 1, r - 2
+            if 0 <= norm < TILES:
+                add_bias(norm)
+            if ahead < TILES:
+                transpose_h(ahead, 0)
+            if 0 <= norm < TILES:
+                deviation(norm)
+            if ahead < TILES:
+                transpose_h(ahead, 1)
+            if 0 <= back < TILES:
+                transpose_n(back)
+            if r < TILES:
+                multiply(r)
+            if 0 <= back < TILES:
+                finish(back)
+            if 0 <= norm < TILES:
+                normalise(norm)
+            if ahead < TILES:
+                quantise_h(ahead)

@@ -26,7 +26,9 @@ TILES_PER_IMAGE = IMAGE // P
 WORDS_PASS = K_PASS // 2
 PASSES_PER_BANK = 2
 BLOCK = 32
+WARM_MATMULS = 3
 LEAD = 2
+LAG = 4
 EPS = 1e-5
 
 FLOPS = 2 * BATCH * IMAGE * K * CHANNELS
@@ -43,7 +45,7 @@ def tile_transformerconvblock_pc_kernel(
     with ExitStack() as ctx:
         const = ctx.enter_context(tc.tile_pool(name="const", bufs=1))
         h_pool = ctx.enter_context(tc.tile_pool(name="h", bufs=TILES))
-        work = ctx.enter_context(tc.tile_pool(name="work", bufs=3))
+        work = ctx.enter_context(tc.tile_pool(name="work", bufs=4))
         stats = ctx.enter_context(tc.tile_pool(name="stats", bufs=3))
         ps_h = ctx.enter_context(tc.psum_pool(name="ps_h", bufs=4))
         ps_acc = ctx.enter_context(tc.psum_pool(name="ps_acc", bufs=2))
@@ -51,6 +53,14 @@ def tile_transformerconvblock_pc_kernel(
 
         w_scales = const.tile([P, PASSES, CHANNELS], U8, align_bytes=64)
         nc.vector.memset(w_scales[:].rearrange("p g n -> p (g n)").bitcast(I32), 0)
+
+        ones = const.tile([P, P], BF16)
+        nc.vector.memset(ones[:], 1.0)
+        zeroes = const.tile([P, CHANNELS], BF16)
+        nc.vector.memset(zeroes[:], 0.0)
+        warm_ps = ps_n.tile([P, CHANNELS], F32, tag="n_t")
+        for i in range(WARM_MATMULS):
+            nc.tensor.matmul(out=warm_ps[:], lhsT=ones[:], rhs=zeroes[:], start=True, stop=True)
 
         col = const.tile([P, BLOCK], F32, align_bytes=64)
         for c in range(4):
@@ -110,7 +120,7 @@ def tile_transformerconvblock_pc_kernel(
         one = const.tile([P, 1], F32)
         nc.vector.memset(one[:], 1.0)
         table_warm = const.tile([P, 1], F32)
-        nc.scalar.activation(out=table_warm[:], in_=one[:], func=ACT.Sqrt)
+        nc.scalar.activation(out=table_warm[:], in_=one[:], func=ACT.Abs_reciprocal_sqrt)
 
         var_scale = const.tile([P, 1], F32)
         nc.vector.tensor_scalar(
@@ -124,7 +134,7 @@ def tile_transformerconvblock_pc_kernel(
         nc.vector.tensor_scalar(out=shift[:], in0=ln_b[:], scalar1=s_norm[:, 0:1], scalar2=None, op0=ALU.mult)
 
         grouped_of, codes_of, planes_of, acc_of = {}, {}, {}, {}
-        v_of, neg_mean_of, dev_of, n_of, n_t_of = {}, {}, {}, {}, {}
+        v_of, neg_mean_of, inv_dev_of, n_of, n_t_of = {}, {}, {}, {}, {}
 
         def transpose_h(t, bank):
             if bank == 0:
@@ -192,19 +202,19 @@ def tile_transformerconvblock_pc_kernel(
                 scale=1.0,
                 accum_out=sq_sum[:],
             )
-            dev = stats.tile([P, 1], F32)
-            nc.scalar.activation(out=dev[:], in_=sq_sum[:], func=ACT.Sqrt, bias=EPS, scale=var_scale[:, 0:1])
-            dev_of[t] = dev
+            inv_dev = stats.tile([P, 1], F32)
+            nc.scalar.activation(
+                out=inv_dev[:], in_=sq_sum[:], func=ACT.Abs_reciprocal_sqrt, bias=EPS, scale=var_scale[:, 0:1]
+            )
+            inv_dev_of[t] = inv_dev
 
         def normalise(t):
-            inv_dev = stats.tile([P, 1], F32)
-            nc.vector.reciprocal(out=inv_dev[:], in_=dev_of[t][:])
             n = work.tile([P, CH_PER_PART, P], F32)
             nc.vector.tensor_scalar(
                 out=n[:].rearrange("p j cc -> p (j cc)"),
                 in0=v_of[t][:].rearrange("p j cc -> p (j cc)"),
                 scalar1=neg_mean_of[t][:, 0:1],
-                scalar2=inv_dev[:, 0:1],
+                scalar2=inv_dev_of[t][:, 0:1],
                 op0=ALU.add,
                 op1=ALU.mult,
             )
@@ -239,15 +249,13 @@ def tile_transformerconvblock_pc_kernel(
             transpose_h(t, 1)
             quantise_h(t)
 
-        ones = const.tile([P, P], BF16)
-        nc.vector.memset(ones[:], 1.0)
         bias_ps = ps_acc.tile([P, CHANNELS], F32, tag="acc")
         nc.tensor.matmul(out=bias_ps[:], lhsT=ones[:], rhs=bias_row[:], start=True, stop=True)
         bias_all = const.tile([P, CH_PER_PART, P], F32)
         nc.vector.tensor_copy(out=bias_all[:], in_=bias_ps[:].rearrange("p (cc j) -> p j cc", j=CH_PER_PART))
 
-        for r in range(TILES + 2):
-            ahead, norm, back = r + LEAD, r - 1, r - 2
+        for r in range(TILES + LAG):
+            ahead, norm, back = r + LEAD, r - 1, r - LAG
             if 0 <= norm < TILES:
                 add_bias(norm)
             if ahead < TILES:

@@ -26,7 +26,7 @@ TILES_PER_IMAGE = IMAGE // P
 WORDS_PASS = K_PASS // 2
 PASSES_PER_BANK = 2
 BLOCK = 32
-WARM_MATMULS = 3
+WARM_MATMULS = 4
 LEAD = 2
 LAG = 4
 EPS = 1e-5
@@ -58,9 +58,6 @@ def tile_transformerconvblock_pc_kernel(
         nc.vector.memset(ones[:], 1.0)
         zeroes = const.tile([P, CHANNELS], BF16)
         nc.vector.memset(zeroes[:], 0.0)
-        warm_ps = ps_n.tile([P, CHANNELS], F32, tag="n_t")
-        for i in range(WARM_MATMULS):
-            nc.tensor.matmul(out=warm_ps[:], lhsT=ones[:], rhs=zeroes[:], start=True, stop=True)
 
         col = const.tile([P, BLOCK], F32, align_bytes=64)
         for c in range(4):
@@ -244,10 +241,19 @@ def tile_transformerconvblock_pc_kernel(
                 )
             nc.sync.dma_start(out=out_view[image][:, :, pixels], in_=res[:])
 
-        for t in range(LEAD):
-            transpose_h(t, 0)
-            transpose_h(t, 1)
-            quantise_h(t)
+        warm_ps = ps_n.tile([P, CHANNELS], F32, tag="n_t")
+
+        def keep_clock():
+            nc.tensor.matmul(out=warm_ps[:], lhsT=ones[:], rhs=zeroes[:], start=True, stop=True)
+
+        with tc.manual_schedule():
+            for i in range(WARM_MATMULS):
+                keep_clock()
+            for t in range(LEAD):
+                for bank in range(PASSES // PASSES_PER_BANK):
+                    transpose_h(t, bank)
+                    keep_clock()
+                quantise_h(t)
 
         bias_ps = ps_acc.tile([P, CHANNELS], F32, tag="acc")
         nc.tensor.matmul(out=bias_ps[:], lhsT=ones[:], rhs=bias_row[:], start=True, stop=True)

@@ -239,7 +239,7 @@ def tile_transformerconvblock_pc_kernel(
                 nc.scalar.activation(
                     out=res[:, j, :], in_=res[:, j, :], func=ACT.Relu, bias=shift[:, j : j + 1], scale=1.0
                 )
-            nc.sync.dma_start(out=out_view[image][:, :, pixels], in_=res[:])
+                nc.sync.dma_start(out=out_view[image][:, j, pixels], in_=res[:, j, :])
 
         warm_ps = ps_n.tile([P, CHANNELS], F32, tag="n_t")
 
@@ -274,9 +274,9 @@ def tile_transformerconvblock_pc_kernel(
                 transpose_n(back)
             if r < TILES:
                 multiply(r)
-            if 0 <= back < TILES:
-                finish(back)
             if 0 <= norm < TILES:
                 normalise(norm)
+            if 0 <= back < TILES:
+                finish(back)
             if ahead < TILES:
                 quantise_h(ahead)

@@ -207,7 +207,8 @@ def tile_transformerconvblock_pc_kernel(
 
         def normalise(t):
             n = work.tile([P, CH_PER_PART, P], F32)
-            nc.vector.tensor_scalar(
+            engine = nc.gpsimd if t < TILES - 1 else nc.vector
+            engine.tensor_scalar(
                 out=n[:].rearrange("p j cc -> p (j cc)"),
                 in0=v_of[t][:].rearrange("p j cc -> p (j cc)"),
                 scalar1=neg_mean_of[t][:, 0:1],

@@ -95,11 +95,10 @@ def tile_transformerconvblock_pc_kernel(
                 out=w_scales[32 * quad : 32 * quad + 4, :, :].bitcast(I32),
                 in_=scale_rows[:, 4 * quad : 4 * quad + 4, :].rearrange("g r n -> r g n"),
             )
-        load_h(2)
+        for t in range(2, TILES):
+            load_h(t)
         x_sb = const.tile([P, BATCH, CH_PER_PART, IMAGE], BF16)
         nc.sync.dma_start(out=x_sb[:], in_=x_view)
-        for t in range(3, TILES):
-            load_h(t)
 
         bias_row = const.tile([P, CHANNELS], BF16)
         nc.vector.memset(bias_row[:], 0.0)

@@ -120,7 +120,7 @@ def tile_transformerconvblock_pc_kernel(
 
         var_scale = const.tile([P, 1], F32)
         nc.vector.tensor_scalar(
-            out=var_scale[:], in0=s_ffn[:], scalar1=s_ffn[:, 0:1], scalar2=1.0 / CHANNELS, op0=ALU.mult, op1=ALU.mult
+            out=var_scale[:], in0=s_ffn[:], scalar1=s_ffn[:, 0:1], scalar2=1.0 / CHANNELS**3, op0=ALU.mult, op1=ALU.mult
         )
         gain = const.tile([P, CH_PER_PART], F32)
         nc.vector.tensor_scalar(
@@ -130,7 +130,7 @@ def tile_transformerconvblock_pc_kernel(
         nc.vector.tensor_scalar(out=shift[:], in0=ln_b[:], scalar1=s_norm[:, 0:1], scalar2=None, op0=ALU.mult)
 
         grouped_of, codes_of, planes_of, acc_of = {}, {}, {}, {}
-        v_of, neg_mean_of, inv_dev_of, n_of, n_t_of = {}, {}, {}, {}, {}
+        v_of, v_sum_of, inv_dev_of, n_of, n_t_of = {}, {}, {}, {}, {}
 
         def transpose_h(t, bank):
             if bank == 0:
@@ -183,9 +183,7 @@ def tile_transformerconvblock_pc_kernel(
                 op1=ALU.add,
                 accum_out=v_sum[:],
             )
-            neg_mean = stats.tile([P, 1], F32)
-            nc.vector.tensor_scalar(out=neg_mean[:], in0=v_sum[:], scalar1=-1.0 / CHANNELS, scalar2=None, op0=ALU.mult)
-            v_of[t], neg_mean_of[t] = v, neg_mean
+            v_of[t], v_sum_of[t] = v, v_sum
 
         def deviation(t):
             squares = work.tile([P, CHANNELS], F32)
@@ -194,8 +192,8 @@ def tile_transformerconvblock_pc_kernel(
                 out=squares[:],
                 in_=v_of[t][:].rearrange("p j cc -> p (j cc)"),
                 func=ACT.Square,
-                bias=neg_mean_of[t][:, 0:1],
-                scale=1.0,
+                bias=v_sum_of[t][:, 0:1],
+                scale=-float(CHANNELS),
                 accum_out=sq_sum[:],
             )
             inv_dev = stats.tile([P, 1], F32)
@@ -206,15 +204,22 @@ def tile_transformerconvblock_pc_kernel(
 
         def normalise(t):
             n = work.tile([P, CH_PER_PART, P], F32)
-            engine = nc.gpsimd if t < TILES - 1 else nc.vector
+            last = t == TILES - 1
+            engine = nc.vector if last else nc.gpsimd
+            neg_mean = stats.tile([P, 1], F32)
             engine.tensor_scalar(
-                out=n[:].rearrange("p j cc -> p (j cc)"),
-                in0=v_of[t][:].rearrange("p j cc -> p (j cc)"),
-                scalar1=neg_mean_of[t][:, 0:1],
-                scalar2=inv_dev_of[t][:, 0:1],
-                op0=ALU.add,
-                op1=ALU.mult,
+                out=neg_mean[:], in0=v_sum_of[t][:], scalar1=-1.0 / CHANNELS, scalar2=0.0, op0=ALU.mult, op1=ALU.add
             )
+            run = 1 if last else CH_PER_PART
+            for j in range(0, CH_PER_PART, run):
+                engine.tensor_scalar(
+                    out=n[:, j : j + run, :].rearrange("p j cc -> p (j cc)"),
+                    in0=v_of[t][:, j : j + run, :].rearrange("p j cc -> p (j cc)"),
+                    scalar1=neg_mean[:, 0:1],
+                    scalar2=inv_dev_of[t][:, 0:1],
+                    op0=ALU.add,
+                    op1=ALU.mult,
+                )
             n_of[t] = n
 
         def transpose_n(t):
@@ -260,8 +265,11 @@ def tile_transformerconvblock_pc_kernel(
         bias_all = const.tile([P, CH_PER_PART, P], F32)
         nc.vector.tensor_copy(out=bias_all[:], in_=bias_ps[:].rearrange("p (cc j) -> p j cc", j=CH_PER_PART))
 
+        backs = {r: [r - LAG] for r in range(LAG, TILES + LAG)}
+        backs[TILES - 2] = backs[TILES - 2] + backs[TILES - 1]
+        backs[TILES - 1] = []
         for r in range(TILES + LAG):
-            ahead, norm, back = r + LEAD, r - 1, r - LAG
+            ahead, norm = r + LEAD, r - 1
             if 0 <= norm < TILES:
                 add_bias(norm)
             if ahead < TILES:
@@ -270,13 +278,13 @@ def tile_transformerconvblock_pc_kernel(
                 deviation(norm)
             if ahead < TILES:
                 transpose_h(ahead, 1)
-            if 0 <= back < TILES:
+            for back in backs.get(r, []):
                 transpose_n(back)
             if r < TILES:
                 multiply(r)
             if 0 <= norm < TILES:
                 normalise(norm)
-            if 0 <= back < TILES:
+            for back in backs.get(r, []):
                 finish(back)
             if ahead < TILES:
                 quantise_h(ahead)

@@ -51,35 +51,39 @@ def tile_transformerconvblock_pc_kernel(
         ps_acc = ctx.enter_context(tc.psum_pool(name="ps_acc", bufs=2))
         ps_n = ctx.enter_context(tc.psum_pool(name="ps_n", bufs=2))
 
-        w_scales = const.tile([P, PASSES, CHANNELS], U8, align_bytes=64)
-        nc.vector.memset(w_scales[:].rearrange("p g n -> p (g n)").bitcast(I32), 0)
-
-        ones = const.tile([P, P], BF16)
-        nc.vector.memset(ones[:], 1.0)
-        zeroes = const.tile([P, CHANNELS], BF16)
-        nc.vector.memset(zeroes[:], 0.0)
-
-        col = const.tile([P, BLOCK], F32, align_bytes=64)
-        for c in range(4):
-            nc.vector.memset(col[:, c : c + 1], float(c))
-        for width in (4, 8, 16):
-            nc.vector.tensor_scalar_add(out=col[:, width : 2 * width], in0=col[:, 0:width], scalar1=float(width))
-        row = const.tile([P, BLOCK], F32, align_bytes=64)
-        nc.vector.transpose(out=row[:], in_=col[:])
-        diagonal = const.tile([P, BLOCK], F32)
-        nc.vector.tensor_tensor(out=diagonal[:], in0=col[:], in1=row[:], op=ALU.is_equal)
+        unit = const.tile([P, BLOCK], F32, align_bytes=64)
+        nc.vector.memset(unit[:], 1.0)
         ident = const.tile([P, P], F32)
         nc.vector.memset(ident[:], 0.0)
+        col = const.tile([P, BLOCK], F32, align_bytes=64)
+        nc.vector.tensor_tensor_scan(
+            out=col[:], data0=unit[:], data1=unit[:], initial=0.0, op0=ALU.mult, op1=ALU.add
+        )
+        row = const.tile([P, BLOCK], F32, align_bytes=64)
+        nc.vector.transpose(out=row[:], in_=col[:])
         for first in range(0, P, BLOCK):
             block = slice(first, first + BLOCK)
-            nc.vector.tensor_copy(out=ident[block, block], in_=diagonal[block, :])
+            nc.vector.tensor_tensor(out=ident[block, block], in0=col[block, :], in1=row[block, :], op=ALU.is_equal)
+
+        table_warm = const.tile([P, 1], F32)
+        nc.scalar.activation(out=table_warm[:], in_=unit[:, 0:1], func=ACT.Abs_reciprocal_sqrt)
+
+        zeroes = const.tile([P, CHANNELS], BF16)
+        nc.gpsimd.memset(zeroes[:].bitcast(F32), 0.0)
+        ones = const.tile([P, P], BF16)
+        nc.gpsimd.memset(ones[:], 1.0)
+        w_scales = const.tile([P, PASSES, CHANNELS], U8, align_bytes=64)
+        nc.gpsimd.memset(w_scales[:].rearrange("p g n -> p (g n)").bitcast(I32), 0)
+        bias_row = const.tile([P, CHANNELS], BF16)
+        nc.gpsimd.memset(bias_row[:].bitcast(F32), 0.0)
 
         h_sb = {}
 
         def load_h(t):
             h_tile = h_pool.tile([P, K], BF16)
-            for half in range(2):
-                cols = slice(half * K // 2, (half + 1) * K // 2)
+            pieces = 1 if t == 1 else 2
+            for piece in range(pieces):
+                cols = slice(piece * K // pieces, (piece + 1) * K // pieces)
                 nc.sync.dma_start(out=h_tile[:, cols], in_=h_rows[t * P : (t + 1) * P, cols])
             h_sb[t] = h_tile
 
@@ -100,34 +104,27 @@ def tile_transformerconvblock_pc_kernel(
         x_sb = const.tile([P, BATCH, CH_PER_PART, IMAGE], BF16)
         nc.sync.dma_start(out=x_sb[:], in_=x_view)
 
-        bias_row = const.tile([P, CHANNELS], BF16)
-        nc.vector.memset(bias_row[:], 0.0)
         nc.scalar.dma_start(out=bias_row[0:1, :], in_=ffn2_b.unsqueeze(0))
         s_ffn = const.tile([P, 1], BF16)
-        nc.scalar.dma_start(out=s_ffn[:], in_=scale_ffn.partition_broadcast(P))
+        nc.gpsimd.dma_start(out=s_ffn[:], in_=scale_ffn.partition_broadcast(P))
         s_norm = const.tile([P, 1], BF16)
-        nc.scalar.dma_start(out=s_norm[:], in_=scale_norm2.partition_broadcast(P))
+        nc.gpsimd.dma_start(out=s_norm[:], in_=scale_norm2.partition_broadcast(P))
         ln_w = const.tile([P, CH_PER_PART], BF16)
-        nc.scalar.dma_start(out=ln_w[:], in_=ln2_w.rearrange("(cc j) -> cc j", j=CH_PER_PART))
+        nc.gpsimd.dma_start(out=ln_w[:], in_=ln2_w.rearrange("(cc j) -> cc j", j=CH_PER_PART))
         ln_b = const.tile([P, CH_PER_PART], BF16)
-        nc.scalar.dma_start(out=ln_b[:], in_=ln2_b.rearrange("(cc j) -> cc j", j=CH_PER_PART))
+        nc.gpsimd.dma_start(out=ln_b[:], in_=ln2_b.rearrange("(cc j) -> cc j", j=CH_PER_PART))
 
-
-        one = const.tile([P, 1], F32)
-        nc.vector.memset(one[:], 1.0)
-        table_warm = const.tile([P, 1], F32)
-        nc.scalar.activation(out=table_warm[:], in_=one[:], func=ACT.Abs_reciprocal_sqrt)
 
         var_scale = const.tile([P, 1], F32)
-        nc.vector.tensor_scalar(
+        nc.gpsimd.tensor_scalar(
             out=var_scale[:], in0=s_ffn[:], scalar1=s_ffn[:, 0:1], scalar2=1.0 / CHANNELS**3, op0=ALU.mult, op1=ALU.mult
         )
         gain = const.tile([P, CH_PER_PART], F32)
-        nc.vector.tensor_scalar(
+        nc.gpsimd.tensor_scalar(
             out=gain[:], in0=ln_w[:], scalar1=s_norm[:, 0:1], scalar2=s_ffn[:, 0:1], op0=ALU.mult, op1=ALU.mult
         )
         shift = const.tile([P, CH_PER_PART], F32)
-        nc.vector.tensor_scalar(out=shift[:], in0=ln_b[:], scalar1=s_norm[:, 0:1], scalar2=None, op0=ALU.mult)
+        nc.gpsimd.tensor_scalar(out=shift[:], in0=ln_b[:], scalar1=s_norm[:, 0:1], scalar2=0.0, op0=ALU.mult, op1=ALU.add)
 
         grouped_of, codes_of, planes_of, acc_of = {}, {}, {}, {}
         v_of, v_sum_of, inv_dev_of, n_of, n_t_of = {}, {}, {}, {}, {}

@@ -27,8 +27,9 @@ WORDS_PASS = K_PASS // 2
 PASSES_PER_BANK = 2
 BLOCK = 32
 WARM_MATMULS = 4
-LEAD = 2
+LEAD = 3
 LAG = 4
+PASSES_PER_LOAD = 2
 EPS = 1e-5
 
 FLOPS = 2 * BATCH * IMAGE * K * CHANNELS
@@ -55,6 +56,8 @@ def tile_transformerconvblock_pc_kernel(
         nc.vector.memset(unit[:], 1.0)
         ident = const.tile([P, P], F32)
         nc.vector.memset(ident[:], 0.0)
+        w_scales = const.tile([P, PASSES, CHANNELS], U8, align_bytes=64)
+        nc.vector.memset(w_scales[:].rearrange("p g n -> p (g n)").bitcast(I32), 0)
         col = const.tile([P, BLOCK], F32, align_bytes=64)
         nc.vector.tensor_tensor_scan(
             out=col[:], data0=unit[:], data1=unit[:], initial=0.0, op0=ALU.mult, op1=ALU.add
@@ -72,8 +75,6 @@ def tile_transformerconvblock_pc_kernel(
         nc.gpsimd.memset(zeroes[:].bitcast(F32), 0.0)
         ones = const.tile([P, P], BF16)
         nc.gpsimd.memset(ones[:], 1.0)
-        w_scales = const.tile([P, PASSES, CHANNELS], U8, align_bytes=64)
-        nc.gpsimd.memset(w_scales[:].rearrange("p g n -> p (g n)").bitcast(I32), 0)
         bias_row = const.tile([P, CHANNELS], BF16)
         nc.gpsimd.memset(bias_row[:].bitcast(F32), 0.0)
 
@@ -81,17 +82,14 @@ def tile_transformerconvblock_pc_kernel(
 
         def load_h(t):
             h_tile = h_pool.tile([P, K], BF16)
-            pieces = 1 if t == 1 else 2
+            pieces = 1 if t < LEAD else 2
             for piece in range(pieces):
                 cols = slice(piece * K // pieces, (piece + 1) * K // pieces)
                 nc.sync.dma_start(out=h_tile[:, cols], in_=h_rows[t * P : (t + 1) * P, cols])
             h_sb[t] = h_tile
 
-        load_h(0)
-        load_h(1)
-
-        w_words = const.tile([P, PASSES, 2 * CHANNELS], U8, align_bytes=64)
-        nc.sync.dma_start(out=w_words[:].bitcast(I32), in_=ffn2_w_words.bitcast(I32).rearrange("g p n -> p g n"))
+        for t in range(LEAD):
+            load_h(t)
 
         scale_rows = ffn2_w_scales.bitcast(I32)
         for quad in range(4):
@@ -99,7 +97,14 @@ def tile_transformerconvblock_pc_kernel(
                 out=w_scales[32 * quad : 32 * quad + 4, :, :].bitcast(I32),
                 in_=scale_rows[:, 4 * quad : 4 * quad + 4, :].rearrange("g r n -> r g n"),
             )
-        for t in range(2, TILES):
+
+        word_rows = ffn2_w_words.bitcast(I32).rearrange("g p n -> p g n")
+        w_words = []
+        for first in range(0, PASSES, PASSES_PER_LOAD):
+            w_part = const.tile([P, PASSES_PER_LOAD, 2 * CHANNELS], U8, align_bytes=64, name="w_words" + str(first))
+            nc.sync.dma_start(out=w_part[:].bitcast(I32), in_=word_rows[:, first : first + PASSES_PER_LOAD, :])
+            w_words.append(w_part)
+        for t in range(LEAD, TILES):
             load_h(t)
         x_sb = const.tile([P, BATCH, CH_PER_PART, IMAGE], BF16)
         nc.sync.dma_start(out=x_sb[:], in_=x_view)
@@ -140,7 +145,8 @@ def tile_transformerconvblock_pc_kernel(
                 for u in range(2):
                     nc.tensor.transpose(h_t[:, gg, u, :], h_words[:, first + u : first + WORDS_PASS : 2], ident[:])
             width = PASSES_PER_BANK * WORDS_PASS
-            nc.scalar.copy(
+            copy = nc.vector.tensor_copy if t < LEAD and bank == 1 else nc.scalar.copy
+            copy(
                 out=grouped_of[t][:]
                 .bitcast(F32)[:, bank * width : (bank + 1) * width]
                 .rearrange("p (g r u) -> p g r u", g=PASSES_PER_BANK, u=2),
@@ -161,7 +167,7 @@ def tile_transformerconvblock_pc_kernel(
                     out=acc[:],
                     lhsT=codes_of[t][:, pixels].bitcast(FP8X4),
                     lhsT_scale=planes_of[t][:, pixels],
-                    rhs=w_words[:, g, :].bitcast(FP4X4),
+                    rhs=w_words[g // PASSES_PER_LOAD][:, g % PASSES_PER_LOAD, :].bitcast(FP4X4),
                     rhs_scale=w_scales[:, g, :],
                     start=(g == 0),
                     stop=(g == PASSES - 1),
@@ -254,10 +260,10 @@ def tile_transformerconvblock_pc_kernel(
             for t in range(LEAD):
                 for bank in range(PASSES // PASSES_PER_BANK):
                     transpose_h(t, bank)
-                    keep_clock()
+                keep_clock()
                 quantise_h(t)
 
-        bias_ps = ps_acc.tile([P, CHANNELS], F32, tag="acc")
+        bias_ps = ps_n.tile([P, CHANNELS], F32, tag="n_t")
         nc.tensor.matmul(out=bias_ps[:], lhsT=ones[:], rhs=bias_row[:], start=True, stop=True)
         bias_all = const.tile([P, CH_PER_PART, P], F32)
         nc.vector.tensor_copy(out=bias_all[:], in_=bias_ps[:].rearrange("p (cc j) -> p j cc", j=CH_PER_PART))

@@ -28,7 +28,7 @@ PASSES_PER_BANK = 2
 BLOCK = 32
 WARM_MATMULS = 4
 LEAD = 3
-LAG = 4
+LAG = 3
 PASSES_PER_LOAD = 2
 EPS = 1e-5
 
@@ -268,10 +268,8 @@ def tile_transformerconvblock_pc_kernel(
         bias_all = const.tile([P, CH_PER_PART, P], F32)
         nc.vector.tensor_copy(out=bias_all[:], in_=bias_ps[:].rearrange("p (cc j) -> p j cc", j=CH_PER_PART))
 
-        backs = {r: [r - LAG] for r in range(LAG, TILES + LAG)}
-        backs[TILES - 2] = backs[TILES - 2] + backs[TILES - 1]
-        backs[TILES - 1] = []
-        for r in range(TILES + LAG):
+        backs = {t + LAG + (t + LAG > TILES - LEAD): [t] for t in range(TILES)}
+        for r in range(max(backs) + 1):
             ahead, norm = r + LEAD, r - 1
             if 0 <= norm < TILES:
                 add_bias(norm)

@@ -145,7 +145,7 @@ def tile_transformerconvblock_pc_kernel(
                 for u in range(2):
                     nc.tensor.transpose(h_t[:, gg, u, :], h_words[:, first + u : first + WORDS_PASS : 2], ident[:])
             width = PASSES_PER_BANK * WORDS_PASS
-            copy = nc.vector.tensor_copy if t < LEAD and bank == 1 else nc.scalar.copy
+            copy = nc.vector.tensor_copy if t <= LEAD and bank == 1 else nc.scalar.copy
             copy(
                 out=grouped_of[t][:]
                 .bitcast(F32)[:, bank * width : (bank + 1) * width]

from contextlib import ExitStack

import concourse.mybir as mybir

F32 = mybir.dt.float32
BF16 = mybir.dt.bfloat16
I32 = mybir.dt.int32
U32 = mybir.dt.uint32
U8 = mybir.dt.uint8
FP8X4 = mybir.dt.float8_e4m3fn_x4
FP4X4 = mybir.dt.float4_e2m1fn_x4
ALU = mybir.AluOpType
ACT = mybir.ActivationFunctionType

P = 128
PACK = 4
K_PASS = P * PACK
K = 2048
PASSES = K // K_PASS
CHANNELS = 512
CH_PER_PART = CHANNELS // P
BATCH = 4
IMAGE = 256
TILES = BATCH * IMAGE // P
TILES_PER_IMAGE = IMAGE // P
WORDS_PASS = K_PASS // 2
PASSES_PER_BANK = 2
BLOCK = 32
WARM_MATMULS = 4
LEAD = 3
LAG = 3
PASSES_PER_LOAD = 2
EPS = 1e-5

FLOPS = 2 * BATCH * IMAGE * K * CHANNELS


def tile_transformerconvblock_pc_kernel(
    tc, h, ffn2_w_words, ffn2_w_scales, ffn2_b, scale_ffn, ln2_w, ln2_b, scale_norm2, x, out
):
    nc = tc.nc
    h_rows = h.rearrange("b i j k -> (b i j) k")
    x_view = x.rearrange("b (cc j) i w -> cc b j (i w)", j=CH_PER_PART)
    out_view = out.rearrange("b (cc j) i w -> b cc j (i w)", j=CH_PER_PART)

    with ExitStack() as ctx:
        const = ctx.enter_context(tc.tile_pool(name="const", bufs=1))
        h_pool = ctx.enter_context(tc.tile_pool(name="h", bufs=TILES))
        work = ctx.enter_context(tc.tile_pool(name="work", bufs=4))
        stats = ctx.enter_context(tc.tile_pool(name="stats", bufs=3))
        ps_h = ctx.enter_context(tc.psum_pool(name="ps_h", bufs=4))
        ps_acc = ctx.enter_context(tc.psum_pool(name="ps_acc", bufs=2))
        ps_n = ctx.enter_context(tc.psum_pool(name="ps_n", bufs=2))

        unit = const.tile([P, BLOCK], F32, align_bytes=64)
        nc.vector.memset(unit[:], 1.0)
        ident = const.tile([P, P], F32)
        nc.vector.memset(ident[:], 0.0)
        w_scales = const.tile([P, PASSES, CHANNELS], U8, align_bytes=64)
        nc.vector.memset(w_scales[:].rearrange("p g n -> p (g n)").bitcast(I32), 0)
        col = const.tile([P, BLOCK], F32, align_bytes=64)
        nc.vector.tensor_tensor_scan(
            out=col[:], data0=unit[:], data1=unit[:], initial=0.0, op0=ALU.mult, op1=ALU.add
        )
        row = const.tile([P, BLOCK], F32, align_bytes=64)
        nc.vector.transpose(out=row[:], in_=col[:])
        for first in range(0, P, BLOCK):
            block = slice(first, first + BLOCK)
            nc.vector.tensor_tensor(out=ident[block, block], in0=col[block, :], in1=row[block, :], op=ALU.is_equal)

        table_warm = const.tile([P, 1], F32)
        nc.scalar.activation(out=table_warm[:], in_=unit[:, 0:1], func=ACT.Abs_reciprocal_sqrt)

        zeroes = const.tile([P, CHANNELS], BF16)
        nc.gpsimd.memset(zeroes[:].bitcast(F32), 0.0)
        ones = const.tile([P, P], BF16)
        nc.gpsimd.memset(ones[:], 1.0)
        bias_row = const.tile([P, CHANNELS], BF16)
        nc.gpsimd.memset(bias_row[:].bitcast(F32), 0.0)

        h_sb = {}

        def load_h(t):
            h_tile = h_pool.tile([P, K], BF16)
            pieces = 1 if t < LEAD else 2
            for piece in range(pieces):
                cols = slice(piece * K // pieces, (piece + 1) * K // pieces)
                nc.sync.dma_start(out=h_tile[:, cols], in_=h_rows[t * P : (t + 1) * P, cols])
            h_sb[t] = h_tile

        for t in range(LEAD):
            load_h(t)

        scale_rows = ffn2_w_scales.bitcast(I32)
        for quad in range(4):
            nc.sync.dma_start(
                out=w_scales[32 * quad : 32 * quad + 4, :, :].bitcast(I32),
                in_=scale_rows[:, 4 * quad : 4 * quad + 4, :].rearrange("g r n -> r g n"),
            )

        word_rows = ffn2_w_words.bitcast(I32).rearrange("g p n -> p g n")
        w_words = []
        for first in range(0, PASSES, PASSES_PER_LOAD):
            w_part = const.tile([P, PASSES_PER_LOAD, 2 * CHANNELS], U8, align_bytes=64, name="w_words" + str(first))
            nc.sync.dma_start(out=w_part[:].bitcast(I32), in_=word_rows[:, first : first + PASSES_PER_LOAD, :])
            w_words.append(w_part)
        for t in range(LEAD, TILES):
            load_h(t)
        x_sb = const.tile([P, BATCH, CH_PER_PART, IMAGE], BF16)
        nc.sync.dma_start(out=x_sb[:], in_=x_view)

        nc.scalar.dma_start(out=bias_row[0:1, :], in_=ffn2_b.unsqueeze(0))
        s_ffn = const.tile([P, 1], BF16)
        nc.gpsimd.dma_start(out=s_ffn[:], in_=scale_ffn.partition_broadcast(P))
        s_norm = const.tile([P, 1], BF16)
        nc.gpsimd.dma_start(out=s_norm[:], in_=scale_norm2.partition_broadcast(P))
        ln_w = const.tile([P, CH_PER_PART], BF16)
        nc.gpsimd.dma_start(out=ln_w[:], in_=ln2_w.rearrange("(cc j) -> cc j", j=CH_PER_PART))
        ln_b = const.tile([P, CH_PER_PART], BF16)
        nc.gpsimd.dma_start(out=ln_b[:], in_=ln2_b.rearrange("(cc j) -> cc j", j=CH_PER_PART))


        var_scale = const.tile([P, 1], F32)
        nc.gpsimd.tensor_scalar(
            out=var_scale[:], in0=s_ffn[:], scalar1=s_ffn[:, 0:1], scalar2=1.0 / CHANNELS**3, op0=ALU.mult, op1=ALU.mult
        )
        gain = const.tile([P, CH_PER_PART], F32)
        nc.gpsimd.tensor_scalar(
            out=gain[:], in0=ln_w[:], scalar1=s_norm[:, 0:1], scalar2=s_ffn[:, 0:1], op0=ALU.mult, op1=ALU.mult
        )
        shift = const.tile([P, CH_PER_PART], F32)
        nc.gpsimd.tensor_scalar(out=shift[:], in0=ln_b[:], scalar1=s_norm[:, 0:1], scalar2=0.0, op0=ALU.mult, op1=ALU.add)

        grouped_of, codes_of, planes_of, acc_of = {}, {}, {}, {}
        v_of, v_sum_of, inv_dev_of, n_of, n_t_of = {}, {}, {}, {}, {}

        def transpose_h(t, bank):
            if bank == 0:
                grouped = work.tile([P, K], BF16, align_bytes=64)
                grouped_of[t] = grouped
            h_words = h_sb[t][:].bitcast(F32)
            h_t = ps_h.tile([P, PASSES_PER_BANK, 2, P], F32)
            for gg in range(PASSES_PER_BANK):
                first = (bank * PASSES_PER_BANK + gg) * WORDS_PASS
                for u in range(2):
                    nc.tensor.transpose(h_t[:, gg, u, :], h_words[:, first + u : first + WORDS_PASS : 2], ident[:])
            width = PASSES_PER_BANK * WORDS_PASS
            copy = nc.vector.tensor_copy if t <= LEAD and bank == 1 else nc.scalar.copy
            copy(
                out=grouped_of[t][:]
                .bitcast(F32)[:, bank * width : (bank + 1) * width]
                .rearrange("p (g r u) -> p g r u", g=PASSES_PER_BANK, u=2),
                in_=h_t[:].rearrange("p g u r -> p g r u"),
            )

        def quantise_h(t):
            codes = work.tile([P, PASSES * P], U32, align_bytes=64)
            planes = work.tile([P, PASSES * P], U8, align_bytes=64)
            nc.vector.quantize_mx(out=codes[:].bitcast(FP8X4), scales=planes[:], in_=grouped_of[t][:])
            codes_of[t], planes_of[t] = codes, planes

        def multiply(t):
            acc = ps_acc.tile([P, CHANNELS], F32, tag="acc")
            for g in range(PASSES):
                pixels = slice(g * P, (g + 1) * P)
                nc.tensor.matmul_mx(
                    out=acc[:],
                    lhsT=codes_of[t][:, pixels].bitcast(FP8X4),
                    lhsT_scale=planes_of[t][:, pixels],
                    rhs=w_words[g // PASSES_PER_LOAD][:, g % PASSES_PER_LOAD, :].bitcast(FP4X4),
                    rhs_scale=w_scales[:, g, :],
                    start=(g == 0),
                    stop=(g == PASSES - 1),
                )
            acc_of[t] = acc

        def add_bias(t):
            v = work.tile([P, CH_PER_PART, P], F32)
            v_sum = stats.tile([P, 1], F32)
            nc.vector.scalar_tensor_tensor(
                out=v[:],
                in0=acc_of[t][:].rearrange("p (cc j) -> p j cc", j=CH_PER_PART),
                scalar=1.0,
                in1=bias_all[:],
                op0=ALU.mult,
                op1=ALU.add,
                accum_out=v_sum[:],
            )
            v_of[t], v_sum_of[t] = v, v_sum

        def deviation(t):
            squares = work.tile([P, CHANNELS], F32)
            sq_sum = stats.tile([P, 1], F32)
            nc.scalar.activation(
                out=squares[:],
                in_=v_of[t][:].rearrange("p j cc -> p (j cc)"),
                func=ACT.Square,
                bias=v_sum_of[t][:, 0:1],
                scale=-float(CHANNELS),
                accum_out=sq_sum[:],
            )
            inv_dev = stats.tile([P, 1], F32)
            nc.scalar.activation(
                out=inv_dev[:], in_=sq_sum[:], func=ACT.Abs_reciprocal_sqrt, bias=EPS, scale=var_scale[:, 0:1]
            )
            inv_dev_of[t] = inv_dev

        def normalise(t):
            n = work.tile([P, CH_PER_PART, P], F32)
            last = t == TILES - 1
            engine = nc.vector if last else nc.gpsimd
            neg_mean = stats.tile([P, 1], F32)
            engine.tensor_scalar(
                out=neg_mean[:], in0=v_sum_of[t][:], scalar1=-1.0 / CHANNELS, scalar2=0.0, op0=ALU.mult, op1=ALU.add
            )
            run = 1 if last else CH_PER_PART
            for j in range(0, CH_PER_PART, run):
                engine.tensor_scalar(
                    out=n[:, j : j + run, :].rearrange("p j cc -> p (j cc)"),
                    in0=v_of[t][:, j : j + run, :].rearrange("p j cc -> p (j cc)"),
                    scalar1=neg_mean[:, 0:1],
                    scalar2=inv_dev_of[t][:, 0:1],
                    op0=ALU.add,
                    op1=ALU.mult,
                )
            n_of[t] = n

        def transpose_n(t):
            n_t = ps_n.tile([P, CH_PER_PART, P], F32)
            for j in range(CH_PER_PART):
                nc.tensor.transpose(n_t[:, j, :], n_of[t][:, j, :], ident[:])
            n_t_of[t] = n_t

        def finish(t):
            image, half = divmod(t, TILES_PER_IMAGE)
            pixels = slice(half * P, (half + 1) * P)
            res = work.tile([P, CH_PER_PART, P], F32)
            for j in range(CH_PER_PART):
                nc.vector.scalar_tensor_tensor(
                    out=res[:, j, :],
                    in0=n_t_of[t][:, j, :],
                    scalar=gain[:, j : j + 1],
                    in1=x_sb[:, image, j, pixels],
                    op0=ALU.mult,
                    op1=ALU.add,
                )
                nc.scalar.activation(
                    out=res[:, j, :], in_=res[:, j, :], func=ACT.Relu, bias=shift[:, j : j + 1], scale=1.0
                )
                nc.sync.dma_start(out=out_view[image][:, j, pixels], in_=res[:, j, :])

        warm_ps = ps_n.tile([P, CHANNELS], F32, tag="n_t")

        def keep_clock():
            nc.tensor.matmul(out=warm_ps[:], lhsT=ones[:], rhs=zeroes[:], start=True, stop=True)

        with tc.manual_schedule():
            for i in range(WARM_MATMULS):
                keep_clock()
            for t in range(LEAD):
                for bank in range(PASSES // PASSES_PER_BANK):
                    transpose_h(t, bank)
                keep_clock()
                quantise_h(t)

        bias_ps = ps_n.tile([P, CHANNELS], F32, tag="n_t")
        nc.tensor.matmul(out=bias_ps[:], lhsT=ones[:], rhs=bias_row[:], start=True, stop=True)
        bias_all = const.tile([P, CH_PER_PART, P], F32)
        nc.vector.tensor_copy(out=bias_all[:], in_=bias_ps[:].rearrange("p (cc j) -> p j cc", j=CH_PER_PART))

        backs = {t + LAG + (t + LAG > TILES - LEAD): [t] for t in range(TILES)}
        for r in range(max(backs) + 1):
            ahead, norm = r + LEAD, r - 1
            if 0 <= norm < TILES:
                add_bias(norm)
            if ahead < TILES:
                transpose_h(ahead, 0)
            if 0 <= norm < TILES:
                deviation(norm)
            if ahead < TILES:
                transpose_h(ahead, 1)
            for back in backs.get(r, []):
                transpose_n(back)
            if r < TILES:
                multiply(r)
            if 0 <= norm < TILES:
                normalise(norm)
            for back in backs.get(r, []):
                finish(back)
            if ahead < TILES:
                quantise_h(ahead)
